import numpy as np
import ml_dtypes


def mxq(x, axis, fmt="e4m3"):
    dtype, down = {"e4m3": (ml_dtypes.float8_e4m3fn, 7), "e5m2": (ml_dtypes.float8_e5m2, 14)}[fmt]
    v = np.moveaxis(np.asarray(x, np.float32).astype(ml_dtypes.bfloat16).astype(np.float64), axis, -1)
    blocks = v.reshape(v.shape[:-1] + (-1, 32))
    amax = np.abs(blocks).max(-1, keepdims=True)
    byte = np.maximum(np.where(amax > 0, np.frexp(amax)[1] - 1 + 127, 0) - down, 1)
    scale = np.exp2(byte - 127.0)
    codes = (blocks / scale).astype(np.float32).astype(dtype).astype(np.float64)
    return np.moveaxis((codes * scale).reshape(v.shape), -1, axis)


WIDE = False


def mx_kscale(k):
    if not WIDE:
        return np.ones(k)
    levels = np.array([30, -30])
    if k % 512:
        return np.exp2(np.random.permutation(np.resize(levels, k // 32))).repeat(32)
    a = np.empty((k // 512, 16))
    for p in range(k // 512):
        a[p, :8] = np.random.permutation(np.resize(levels, 8))
        for g in range(8):
            far = levels[np.abs(levels - a[p, g]) >= 10]
            a[p, g + 8] = far[np.random.randint(len(far))]
    return np.exp2(a.ravel()).repeat(32)


BF16 = ml_dtypes.bfloat16


def bf(x):
    return np.asarray(x, np.float32).astype(BF16)


def f64(x):
    return np.asarray(x).astype(np.float64)


E2M1 = np.array([0.0, 0.5, 1.0, 1.5, 2.0, 3.0, 4.0, 6.0, -0.0, -0.5, -1.0, -1.5, -2.0, -3.0, -4.0, -6.0])


def pack_weight(w, fmt):
    k, n = w.shape
    w = f64(bf(w)).reshape(k // 32, 32, n)
    amax = np.abs(w).max(1)
    if fmt == "e4m3":
        byte = np.frexp(amax)[1] - 1 + 127 - 7
    else:
        mant, ex = np.frexp(amax / 6.0)
        byte = np.where(mant > 0.5, ex, ex - 1) + 127
    byte = np.clip(np.where(amax > 0, byte, 1), 1, 254)
    scaled = (w * np.exp2(127.0 - byte)[:, None, :]).reshape(k, n).astype(np.float32)
    by_word = np.ascontiguousarray(scaled.reshape(k // 512, 128, 4, n).transpose(0, 1, 3, 2))
    if fmt == "e4m3":
        words = by_word.astype(ml_dtypes.float8_e4m3fn).view(np.uint8)
    else:
        c = by_word.astype(ml_dtypes.float4_e2m1fn).view(np.uint8) & 0xF
        words = c[..., 0::2] | (c[..., 1::2] << 4)
    return np.ascontiguousarray(words), np.ascontiguousarray(byte.astype(np.uint8).reshape(k // 512, 16, n))


def unpack_weight(words, scales, fmt):
    g, p, n, _ = words.shape
    if fmt == "e4m3":
        vals = np.ascontiguousarray(words).view(ml_dtypes.float8_e4m3fn).astype(np.float64)
    else:
        nib = np.empty((g, p, n, 4), np.uint8)
        nib[..., 0::2] = words & 0xF
        nib[..., 1::2] = words >> 4
        vals = E2M1[nib]
    vals = vals * np.repeat(np.exp2(scales.astype(np.float64) - 127.0), 8, axis=1)[..., None]
    return vals.transpose(0, 1, 3, 2).reshape(g * 512, n)

def pack4(w):
    words, scales = pack_weight(w, "e2m1")
    return words.reshape(words.shape[0], 128, -1), scales


def unpack4(words, scales):
    return unpack_weight(words.reshape(words.shape[0], 128, -1, 2), scales, "e2m1")


B, N, DIM, H, DH, PD = 2, 1024, 1024, 16, 64, 2
E = H * DH
ROT = DH // PD
INV_MIN_FREQ = 2.0 ** 6


def rot_freqs(t):
    inv_freq = 1.0 / (10000.0 ** (np.arange(0, ROT, 2) / ROT))
    f = (t * INV_MIN_FREQ)[..., None] * inv_freq
    return np.concatenate([f, f], axis=-1)


def rotate_half(x):
    x1, x2 = np.split(x, 2, axis=-1)
    return np.concatenate([-x2, x1], axis=-1)


def apply_rotary(t, freqs):
    return t * np.cos(freqs) + rotate_half(t) * np.sin(freqs)


def rope_2d(t, pos):
    fx = rot_freqs(pos[..., 0])[:, None]
    fy = rot_freqs(pos[..., 1])[:, None]
    return np.concatenate([apply_rotary(t[..., :ROT], fx), apply_rotary(t[..., ROT:], fy)], axis=-1)


def setup_inputs():
    s = mx_kscale(DIM)
    u_x = bf(np.random.standard_normal((B, N, DIM)) * s)
    pos_x = bf(np.random.uniform(size=(1, N, PD)))
    Wq = np.random.standard_normal((E, DIM)) / np.sqrt(DIM) / s
    words, scales = pack4(np.ascontiguousarray(Wq.T))
    return {"u_x": u_x,
            "pos_x": pos_x,
            "Wq_words": words,
            "Wq_scales": scales}


def reference(u_x, pos_x, Wq_words, Wq_scales):
    y = mxq(f64(u_x), 2, "e5m2") @ unpack4(Wq_words, Wq_scales)
    q = y.reshape(B, N, H, DH).transpose(0, 2, 1, 3)
    return rope_2d(q, f64(pos_x))

@@ -1,0 +1,181 @@
+import math
+from contextlib import ExitStack
+
+import concourse.mybir as mybir
+from concourse.masks import make_identity
+
+F32 = mybir.dt.float32
+BF16 = mybir.dt.bfloat16
+I32 = mybir.dt.int32
+U32 = mybir.dt.uint32
+U8 = mybir.dt.uint8
+E5X4 = mybir.dt.float8_e5m2_x4
+E2X4 = mybir.dt.float4_e2m1fn_x4
+ALU = mybir.AluOpType
+ACT = mybir.ActivationFunctionType
+
+FLOPS = 2 * 2048 * 1024 * 1024
+
+P = 128
+SLOTS = 8
+TILES = 16
+BANKS = 32
+
+
+def tile_asymetrickernel_pb_kernel(tc, u_x, pos_x, Wq_words, Wq_scales, out):
+    nc = tc.nc
+    with ExitStack() as ctx:
+        keep = ctx.enter_context(tc.tile_pool(name="keep", bufs=1))
+        stage = ctx.enter_context(tc.tile_pool(name="stage", bufs=3))
+        prod = ctx.enter_context(tc.tile_pool(name="prod", bufs=3))
+        psum_t = ctx.enter_context(tc.psum_pool(name="psum_t", bufs=2))
+        psum_a = ctx.enter_context(tc.psum_pool(name="psum_a", bufs=6))
+
+        ident = keep.tile([P, P], F32, name="ident")
+        make_identity(nc, ident[:])
+
+        plane = keep.tile([P, 2, 1024], U8, name="plane", align_bytes=64)
+        w_half = [keep.tile([P, 2, 1024], U8, name="w_half%d" % nh, align_bytes=64) for nh in range(2)]
+        pos = keep.tile([P, 16], BF16, name="pos")
+        x_sb = [keep.tile([P, 1024], BF16, name="x_sb%d" % t, align_bytes=64) for t in range(TILES)]
+        codes = keep.tile([P, TILES, 256], U32, name="codes", align_bytes=64)
+        xscale = keep.tile([P, TILES, 256], U8, name="xscale", align_bytes=64)
+        turns = keep.tile([P, 2, 16, 16], F32, name="turns")
+        whole = keep.tile([P, 2, 16, 16], I32, name="whole")
+        frac = keep.tile([P, 2, 16, 16], F32, name="frac")
+        cos_t = keep.tile([P, 16, 2, 16], F32, name="cos_t")
+        sin_t = keep.tile([P, 16, 2, 16], F32, name="sin_t")
+        zero = keep.tile([P, 1], F32, name="zero")
+        warm = keep.tile([P, 1], F32, name="warm")
+        res = [keep.tile([P, 8, SLOTS, 64], F32, name="res%d" % q) for q in range(4)]
+
+        with tc.manual_schedule():
+            nc.vector.memset(plane[:].bitcast(I32), 0)
+            nc.gpsimd.memset(zero[:], 0.0)
+            nc.scalar.activation(out=warm[:], in_=zero[:], func=ACT.Sin)
+
+            def load_x(t):
+                b, s = divmod(t, SLOTS)
+                nc.sync.dma_start(out=x_sb[t][:], in_=u_x[b].rearrange("(p s) k -> p s k", s=SLOTS)[:, s, :])
+
+            def load_w(nh):
+                nc.sync.dma_start(
+                    out=w_half[nh][:].bitcast(I32),
+                    in_=Wq_words.rearrange("g p n -> p g n")[:, :, 1024 * nh : 1024 * (nh + 1)].bitcast(I32),
+                )
+
+            nc.sync.dma_start(out=pos[:], in_=pos_x[0].rearrange("(p s) d -> p (s d)", s=SLOTS))
+            load_x(0)
+            for q in range(4):
+                nc.sync.dma_start(
+                    out=plane[32 * q : 32 * q + 4, :, :].bitcast(I32),
+                    in_=Wq_scales[:, 4 * q : 4 * q + 4, :].rearrange("g r n -> r g n").bitcast(I32),
+                )
+            load_w(0)
+            for t in range(1, SLOTS):
+                load_x(t)
+            load_w(1)
+            for t in range(SLOTS, TILES):
+                load_x(t)
+
+            def transpose(t):
+                words = x_sb[t][:].bitcast(F32)
+                xt = psum_t.tile([P, 4, P], F32, name="xt", tag="xt")
+                for g in range(2):
+                    for u in range(2):
+                        nc.tensor.transpose(xt[:, 2 * g + u, :], words[:, 256 * g + u : 256 * (g + 1) : 2], ident[:])
+                grouped = stage.tile([P, 1024], BF16, name="grouped", tag="grouped", align_bytes=64)
+                nc.scalar.copy(
+                    out=grouped[:].bitcast(F32).rearrange("p (g r u) -> p g r u", g=2, u=2),
+                    in_=xt[:].rearrange("p (g u) r -> p g r u", u=2),
+                )
+                return grouped
+
+            def quantize(t, grouped):
+                nc.vector.quantize_mx(out=codes[:, t, :].bitcast(E5X4), scales=xscale[:, t, :], in_=grouped[:])
+
+            def multiply(t, nh):
+                acc = psum_a.tile([P, 512], F32, name="acc", tag="acc")
+                for g in range(2):
+                    nc.tensor.matmul_mx(
+                        out=acc[:],
+                        lhsT=codes[:, t, 128 * g : 128 * (g + 1)].bitcast(E5X4),
+                        lhsT_scale=xscale[:, t, 128 * g : 128 * (g + 1)],
+                        rhs=w_half[nh][:, g, :].bitcast(E2X4),
+                        rhs_scale=plane[:, g, 512 * nh : 512 * (nh + 1)],
+                        start=(g == 0),
+                        stop=(g == 1),
+                    )
+                return acc
+
+            def rotate(q, s, acc):
+                a_t = prod.tile([P, 512], F32, name="a_t", tag="a_t")
+                b_t = prod.tile([P, 512], F32, name="b_t", tag="b_t")
+                cos_s = cos_t[:].rearrange("p (s d) f j -> p s (d f j)", d=2)[:, s : s + 1, :]
+                nc.vector.tensor_tensor(
+                    out=a_t[:].rearrange("p (h c) -> p h c", c=64),
+                    in0=acc[:].rearrange("p (h c) -> p h c", c=64),
+                    in1=cos_s.to_broadcast([P, 8, 64]),
+                    op=ALU.mult,
+                )
+                sin_s = sin_t[:].rearrange("p (s d) f j -> p s d f j", d=2)
+                acc5 = acc[:].rearrange("p (h d f j) -> p h d f j", d=2, f=2, j=16)
+                b5 = b_t[:].rearrange("p (h d f j) -> p h d f j", d=2, f=2, j=16)
+                for f in range(2):
+                    nc.vector.tensor_tensor(
+                        out=b5[:, :, :, f, :],
+                        in0=acc5[:, :, :, 1 - f, :],
+                        in1=sin_s[:, s : s + 1, :, f, :].to_broadcast([P, 8, 2, 16]),
+                        op=ALU.mult,
+                    )
+                nc.gpsimd.tensor_tensor(
+                    out=res[q][:, :, s, :],
+                    in0=a_t[:].rearrange("p (h c) -> p h c", c=64),
+                    in1=b_t[:].rearrange("p (h c) -> p h c", c=64),
+                    op=ALU.add,
+                )
+
+            def store(q, s0, s1, h0, h1):
+                b, nh = divmod(q, 2)
+                nc.sync.dma_start(
+                    out=out[b, 8 * nh + h0 : 8 * nh + h1].rearrange("h (p s) c -> p h s c", s=SLOTS)[:, :, s0:s1, :],
+                    in_=res[q][:, h0:h1, s0:s1, :],
+                )
+
+            grouped = {}
+            for t in range(3):
+                grouped[t] = transpose(t)
+
+            for j in range(16):
+                nc.vector.tensor_scalar(
+                    out=turns[:, 1, :, j],
+                    in0=pos[:],
+                    scalar1=64.0 * 10000.0 ** (-j / 16.0) / (2.0 * math.pi),
+                    scalar2=None,
+                    op0=ALU.mult,
+                )
+            nc.vector.tensor_scalar(out=turns[:, 0], in0=turns[:, 1], scalar1=0.25, scalar2=None, op0=ALU.add)
+            quantize(0, grouped[0])
+            nc.vector.tensor_copy(out=whole[:], in_=turns[:])
+            nc.vector.tensor_tensor(out=frac[:], in0=turns[:], in1=whole[:], op=ALU.subtract)
+            quantize(1, grouped[1])
+            for f in range(2):
+                nc.scalar.activation(out=cos_t[:, :, f, :], in_=frac[:, 0], func=ACT.Sin, scale=2.0 * math.pi)
+            nc.scalar.activation(out=sin_t[:, :, 0, :], in_=frac[:, 1], func=ACT.Sin, scale=-2.0 * math.pi)
+            nc.scalar.activation(out=sin_t[:, :, 1, :], in_=frac[:, 1], func=ACT.Sin, scale=2.0 * math.pi)
+
+            for i in range(BANKS):
+                q, s = divmod(i, SLOTS)
+                t = (q // 2) * SLOTS + s
+                acc = multiply(t, q % 2)
+                if i + 3 < TILES:
+                    grouped[i + 3] = transpose(i + 3)
+                if i + 2 < TILES:
+                    quantize(i + 2, grouped[i + 2])
+                rotate(q, s, acc)
+                if q < 3:
+                    if s == SLOTS - 1:
+                        store(q, 0, SLOTS, 0, 4)
+                        store(q, 0, SLOTS, 4, 8)
+                elif s in (3, 5, 6, 7):
+                    store(q, {3: 0, 5: 4, 6: 6, 7: 7}[s], s + 1, 0, 8)

@@ -21,12 +21,18 @@ SLOTS = 8
 TILES = 16
 BANKS = 32
 
+STORES = [(0, 0, 8), (1, 0, 8), (2, 0, 8), (3, 0, 4), (3, 4, 2), (3, 6, 1), (3, 7, 1)]
+ADDS = [(1, "g"), (1, "g"), (2, "g"), (2, "g"), (2, "g"),
+        (2, "g"), (2, "g"), (2, "g"), (2, "g"),
+        (2, "g"), (2, "g"), (2, "g"), (2, "g"),
+        (2, "g"), (2, "g"), (2, "g"), (1, "v"), (1, "v")]
+
 
 def tile_asymetrickernel_pb_kernel(tc, u_x, pos_x, Wq_words, Wq_scales, out):
     nc = tc.nc
     with ExitStack() as ctx:
         keep = ctx.enter_context(tc.tile_pool(name="keep", bufs=1))
-        stage = ctx.enter_context(tc.tile_pool(name="stage", bufs=3))
+        stage = ctx.enter_context(tc.tile_pool(name="stage", bufs=4))
         prod = ctx.enter_context(tc.tile_pool(name="prod", bufs=3))
         psum_t = ctx.enter_context(tc.psum_pool(name="psum_t", bufs=2))
         psum_a = ctx.enter_context(tc.psum_pool(name="psum_a", bufs=6))
@@ -43,11 +49,10 @@ def tile_asymetrickernel_pb_kernel(tc, u_x, pos_x, Wq_words, Wq_scales, out):
         turns = keep.tile([P, 2, 16, 16], F32, name="turns")
         whole = keep.tile([P, 2, 16, 16], I32, name="whole")
         frac = keep.tile([P, 2, 16, 16], F32, name="frac")
-        cos_t = keep.tile([P, 16, 2, 16], F32, name="cos_t")
-        sin_t = keep.tile([P, 16, 2, 16], F32, name="sin_t")
+        tab = keep.tile([P, SLOTS, 2, 64], F32, name="tab")
         zero = keep.tile([P, 1], F32, name="zero")
         warm = keep.tile([P, 1], F32, name="warm")
-        res = [keep.tile([P, 8, SLOTS, 64], F32, name="res%d" % q) for q in range(4)]
+        res = [keep.tile([P, 8, n, 64], F32, name="res%d" % k) for k, (q, s0, n) in enumerate(STORES)]
 
         with tc.manual_schedule():
             nc.vector.memset(plane[:].bitcast(I32), 0)
@@ -78,21 +83,27 @@ def tile_asymetrickernel_pb_kernel(tc, u_x, pos_x, Wq_words, Wq_scales, out):
             for t in range(SLOTS, TILES):
                 load_x(t)
 
-            def transpose(t):
+            def transpose(t, grouped):
                 words = x_sb[t][:].bitcast(F32)
                 xt = psum_t.tile([P, 4, P], F32, name="xt", tag="xt")
                 for g in range(2):
                     for u in range(2):
                         nc.tensor.transpose(xt[:, 2 * g + u, :], words[:, 256 * g + u : 256 * (g + 1) : 2], ident[:])
-                grouped = stage.tile([P, 1024], BF16, name="grouped", tag="grouped", align_bytes=64)
                 nc.scalar.copy(
-                    out=grouped[:].bitcast(F32).rearrange("p (g r u) -> p g r u", g=2, u=2),
+                    out=grouped.bitcast(F32).rearrange("p (g r u) -> p g r u", g=2, u=2),
                     in_=xt[:].rearrange("p (g u) r -> p g r u", u=2),
                 )
-                return grouped
 
-            def quantize(t, grouped):
-                nc.vector.quantize_mx(out=codes[:, t, :].bitcast(E5X4), scales=xscale[:, t, :], in_=grouped[:])
+            def quantize(t, n, grouped):
+                nc.vector.quantize_mx(
+                    out=codes[:, t : t + n, :].rearrange("p a c -> p (a c)").bitcast(E5X4),
+                    scales=xscale[:, t : t + n, :].rearrange("p a c -> p (a c)"),
+                    in_=grouped,
+                )
+
+            def new_pair():
+                pair = stage.tile([P, 2, 1024], BF16, name="pair", tag="pair", align_bytes=64)
+                return pair
 
             def multiply(t, nh):
                 acc = psum_a.tile([P, 512], F32, name="acc", tag="acc")
@@ -108,43 +119,48 @@ def tile_asymetrickernel_pb_kernel(tc, u_x, pos_x, Wq_words, Wq_scales, out):
                     )
                 return acc
 
-            def rotate(q, s, acc):
-                a_t = prod.tile([P, 512], F32, name="a_t", tag="a_t")
-                b_t = prod.tile([P, 512], F32, name="b_t", tag="b_t")
-                cos_s = cos_t[:].rearrange("p (s d) f j -> p s (d f j)", d=2)[:, s : s + 1, :]
+            def products(ab, k, s, acc):
                 nc.vector.tensor_tensor(
-                    out=a_t[:].rearrange("p (h c) -> p h c", c=64),
-                    in0=acc[:].rearrange("p (h c) -> p h c", c=64),
-                    in1=cos_s.to_broadcast([P, 8, 64]),
+                    out=ab[:, :, :, k, :],
+                    in0=acc[:].rearrange("p (o h c) -> p o h c", o=1, c=64).to_broadcast([P, 2, 8, 64]),
+                    in1=tab[:, s].unsqueeze(2).to_broadcast([P, 2, 8, 64]),
                     op=ALU.mult,
                 )
-                sin_s = sin_t[:].rearrange("p (s d) f j -> p s d f j", d=2)
-                acc5 = acc[:].rearrange("p (h d f j) -> p h d f j", d=2, f=2, j=16)
-                b5 = b_t[:].rearrange("p (h d f j) -> p h d f j", d=2, f=2, j=16)
-                for f in range(2):
-                    nc.vector.tensor_tensor(
-                        out=b5[:, :, :, f, :],
-                        in0=acc5[:, :, :, 1 - f, :],
-                        in1=sin_s[:, s : s + 1, :, f, :].to_broadcast([P, 8, 2, 16]),
-                        op=ALU.mult,
-                    )
-                nc.gpsimd.tensor_tensor(
-                    out=res[q][:, :, s, :],
-                    in0=a_t[:].rearrange("p (h c) -> p h c", c=64),
-                    in1=b_t[:].rearrange("p (h c) -> p h c", c=64),
+
+            def add(engine, ab, dest):
+                ab6 = ab[:].rearrange("p r h s (d f j) -> p r h s d f j", d=2, f=2)
+                engine.tensor_tensor(
+                    out=dest.rearrange("p h s (d f j) -> p h s d f j", d=2, f=2),
+                    in0=ab6[:, 0],
+                    in1=ab6[:, 1, :, :, :, ::-1, :],
                     op=ALU.add,
                 )
 
-            def store(q, s0, s1, h0, h1):
+            def store(k, h0, h1):
+                q, s0, n = STORES[k]
                 b, nh = divmod(q, 2)
                 nc.sync.dma_start(
-                    out=out[b, 8 * nh + h0 : 8 * nh + h1].rearrange("h (p s) c -> p h s c", s=SLOTS)[:, :, s0:s1, :],
-                    in_=res[q][:, h0:h1, s0:s1, :],
+                    out=out[b, 8 * nh + h0 : 8 * nh + h1].rearrange("h (p s) c -> p h s c", s=SLOTS)[:, :, s0 : s0 + n, :],
+                    in_=res[k][:, h0:h1, :, :],
                 )
 
-            grouped = {}
-            for t in range(3):
-                grouped[t] = transpose(t)
+            def sines(s0, s1):
+                tab6 = tab[:].rearrange("p s r (d f j) -> p s r d f j", d=2, f=2)
+                fr = frac[:].rearrange("p k (s d) j -> p k s d j", d=2)
+                for f in range(2):
+                    nc.scalar.activation(out=tab6[:, s0:s1, 0, :, f, :], in_=fr[:, 0, s0:s1], func=ACT.Sin, scale=2.0 * math.pi)
+                nc.scalar.activation(out=tab6[:, s0:s1, 1, :, 0, :], in_=fr[:, 1, s0:s1], func=ACT.Sin, scale=2.0 * math.pi)
+                nc.scalar.activation(out=tab6[:, s0:s1, 1, :, 1, :], in_=fr[:, 1, s0:s1], func=ACT.Sin, scale=-2.0 * math.pi)
+
+            pairs = {}
+
+            def prepare(t):
+                if t % 2 == 0:
+                    pairs[t // 2] = new_pair()
+                transpose(t, pairs[t // 2][:, t % 2, :])
+
+            prepare(0)
+            prepare(1)
 
             for j in range(16):
                 nc.vector.tensor_scalar(
@@ -155,27 +171,43 @@ def tile_asymetrickernel_pb_kernel(tc, u_x, pos_x, Wq_words, Wq_scales, out):
                     op0=ALU.mult,
                 )
             nc.vector.tensor_scalar(out=turns[:, 0], in0=turns[:, 1], scalar1=0.25, scalar2=None, op0=ALU.add)
-            quantize(0, grouped[0])
             nc.vector.tensor_copy(out=whole[:], in_=turns[:])
             nc.vector.tensor_tensor(out=frac[:], in0=turns[:], in1=whole[:], op=ALU.subtract)
-            quantize(1, grouped[1])
-            for f in range(2):
-                nc.scalar.activation(out=cos_t[:, :, f, :], in_=frac[:, 0], func=ACT.Sin, scale=2.0 * math.pi)
-            nc.scalar.activation(out=sin_t[:, :, 0, :], in_=frac[:, 1], func=ACT.Sin, scale=-2.0 * math.pi)
-            nc.scalar.activation(out=sin_t[:, :, 1, :], in_=frac[:, 1], func=ACT.Sin, scale=2.0 * math.pi)
+            quantize(0, 1, pairs[0][:, 0, :])
+            quantize(1, 1, pairs[0][:, 1, :])
+            sines(0, 2)
+            prepare(2)
+            sines(2, 4)
 
+            adds = list(ADDS)
+            left = 0
             for i in range(BANKS):
                 q, s = divmod(i, SLOTS)
                 t = (q // 2) * SLOTS + s
                 acc = multiply(t, q % 2)
-                if i + 3 < TILES:
-                    grouped[i + 3] = transpose(i + 3)
-                if i + 2 < TILES:
-                    quantize(i + 2, grouped[i + 2])
-                rotate(q, s, acc)
-                if q < 3:
-                    if s == SLOTS - 1:
-                        store(q, 0, SLOTS, 0, 4)
-                        store(q, 0, SLOTS, 4, 8)
-                elif s in (3, 5, 6, 7):
-                    store(q, {3: 0, 5: 4, 6: 6, 7: 7}[s], s + 1, 0, 8)
+                if i == 0:
+                    prepare(3)
+                    sines(4, SLOTS)
+                if i + 4 < TILES:
+                    prepare(i + 4)
+                if i < 4:
+                    quantize(i + 2, 1, pairs[(i + 2) // 2][:, i % 2, :])
+                elif i + 2 < TILES and i % 2 == 0:
+                    quantize(i + 2, 2, pairs[i // 2 + 1][:].rearrange("p a c -> p (a c)"))
+                if left == 0:
+                    width, who = adds.pop(0)
+                    left = width
+                    first = s
+                    ab = prod.tile([P, 2, 8, width, 64], F32, name="ab", tag="ab")
+                products(ab, s - first, s, acc)
+                left -= 1
+                if left == 0:
+                    k = [n for n, (sq, s0, sn) in enumerate(STORES) if sq == q and s0 <= s < s0 + sn][0]
+                    s0 = STORES[k][1]
+                    add(nc.vector if who == "v" else nc.gpsimd, ab, res[k][:, :, first - s0 : s + 1 - s0, :])
+                    if s + 1 == s0 + STORES[k][2]:
+                        if STORES[k][2] == SLOTS:
+                            store(k, 0, 4)
+                            store(k, 4, 8)
+                        else:
+                            store(k, 0, 8)

@@ -21,11 +21,11 @@ SLOTS = 8
 TILES = 16
 BANKS = 32
 
-STORES = [(0, 0, 8), (1, 0, 8), (2, 0, 8), (3, 0, 4), (3, 4, 2), (3, 6, 1), (3, 7, 1)]
-ADDS = [(1, "g"), (1, "g"), (2, "g"), (2, "g"), (2, "g"),
-        (2, "g"), (2, "g"), (2, "g"), (2, "g"),
-        (2, "g"), (2, "g"), (2, "g"), (2, "g"),
-        (2, "g"), (2, "g"), (2, "g"), (1, "v"), (1, "v")]
+STORES = [(0, 0, 8), (1, 0, 8), (2, 0, 4), (2, 4, 4), (3, 0, 2), (3, 2, 2), (3, 4, 2), (3, 6, 1), (3, 7, 1)]
+A_BANKS = []
+V_ADDS = [30,31]
+ALONE = [0,1]
+LAG = 0
 
 
 def tile_asymetrickernel_pb_kernel(tc, u_x, pos_x, Wq_words, Wq_scales, out):
@@ -35,7 +35,8 @@ def tile_asymetrickernel_pb_kernel(tc, u_x, pos_x, Wq_words, Wq_scales, out):
         stage = ctx.enter_context(tc.tile_pool(name="stage", bufs=4))
         prod = ctx.enter_context(tc.tile_pool(name="prod", bufs=3))
         psum_t = ctx.enter_context(tc.psum_pool(name="psum_t", bufs=2))
-        psum_a = ctx.enter_context(tc.psum_pool(name="psum_a", bufs=6))
+        psum_v = ctx.enter_context(tc.psum_pool(name="psum_v", bufs=5))
+        psum_a = ctx.enter_context(tc.psum_pool(name="psum_a", bufs=1))
 
         ident = keep.tile([P, P], F32, name="ident")
         make_identity(nc, ident[:])
@@ -50,11 +51,35 @@ def tile_asymetrickernel_pb_kernel(tc, u_x, pos_x, Wq_words, Wq_scales, out):
         whole = keep.tile([P, 2, 16, 16], I32, name="whole")
         frac = keep.tile([P, 2, 16, 16], F32, name="frac")
         tab = keep.tile([P, SLOTS, 2, 64], F32, name="tab")
+        dummy = keep.tile([P, 512], BF16, name="dummy")
         zero = keep.tile([P, 1], F32, name="zero")
         warm = keep.tile([P, 1], F32, name="warm")
         res = [keep.tile([P, 8, n, 64], F32, name="res%d" % k) for k, (q, s0, n) in enumerate(STORES)]
 
+        groups = []
+        open_group = {}
+        for i in range(BANKS):
+            q, s = divmod(i, SLOTS)
+            k = [n for n, (sq, s0, sn) in enumerate(STORES) if sq == q and s0 <= s < s0 + sn][0]
+            key = (k, i in A_BANKS)
+            if key in open_group and i not in ALONE:
+                groups[open_group.pop(key)]["banks"].append(i)
+            else:
+                if i not in ALONE:
+                    open_group[key] = len(groups)
+                groups.append({"banks": [i], "store": k, "scalar": i in A_BANKS})
+        group_of = {}
+        for n, grp in enumerate(groups):
+            for i in grp["banks"]:
+                group_of[i] = n
+        last_add = {}
+        for n, grp in enumerate(groups):
+            grp["when"] = grp["banks"][-1] + (LAG if grp["scalar"] else 0)
+        for n in sorted(range(len(groups)), key=lambda m: (groups[m]["when"], m)):
+            last_add[groups[n]["store"]] = n
+
         with tc.manual_schedule():
+            nc.vector.memset(dummy[:], 0.0)
             nc.vector.memset(plane[:].bitcast(I32), 0)
             nc.gpsimd.memset(zero[:], 0.0)
             nc.scalar.activation(out=warm[:], in_=zero[:], func=ACT.Sin)
@@ -105,8 +130,8 @@ def tile_asymetrickernel_pb_kernel(tc, u_x, pos_x, Wq_words, Wq_scales, out):
                 pair = stage.tile([P, 2, 1024], BF16, name="pair", tag="pair", align_bytes=64)
                 return pair
 
-            def multiply(t, nh):
-                acc = psum_a.tile([P, 512], F32, name="acc", tag="acc")
+            def multiply(t, nh, pool):
+                acc = pool.tile([P, 512], F32, name="acc", tag="acc")
                 for g in range(2):
                     nc.tensor.matmul_mx(
                         out=acc[:],
@@ -119,7 +144,7 @@ def tile_asymetrickernel_pb_kernel(tc, u_x, pos_x, Wq_words, Wq_scales, out):
                     )
                 return acc
 
-            def products(ab, k, s, acc):
+            def both_products(ab, k, s, acc):
                 nc.vector.tensor_tensor(
                     out=ab[:, :, :, k, :],
                     in0=acc[:].rearrange("p (o h c) -> p o h c", o=1, c=64).to_broadcast([P, 2, 8, 64]),
@@ -127,14 +152,61 @@ def tile_asymetrickernel_pb_kernel(tc, u_x, pos_x, Wq_words, Wq_scales, out):
                     op=ALU.mult,
                 )
 
-            def add(engine, ab, dest):
-                ab6 = ab[:].rearrange("p r h s (d f j) -> p r h s d f j", d=2, f=2)
-                engine.tensor_tensor(
-                    out=dest.rearrange("p h s (d f j) -> p h s d f j", d=2, f=2),
-                    in0=ab6[:, 0],
-                    in1=ab6[:, 1, :, :, :, ::-1, :],
-                    op=ALU.add,
+            def sine_product(bs, k, s, acc):
+                nc.vector.tensor_tensor(
+                    out=bs[:, :, k, :],
+                    in0=acc[:].rearrange("p (h c) -> p h c", c=64),
+                    in1=tab[:, s, 1:2, :].to_broadcast([P, 8, 64]),
+                    op=ALU.mult,
                 )
+
+            def cosine_product(ap, k, s, acc):
+                ap7 = ap[:].rearrange("p a s (d f j) e -> p a s d f j e", d=2, f=2)
+                acc6 = acc[:].rearrange("p (a e d f j) -> p a e d f j", e=2, d=2, f=2, j=16)
+                for d in range(2):
+                    for j in range(16):
+                        nc.scalar.activation(
+                            out=ap7[:, :, k, d, :, j, :],
+                            in_=acc6[:, :, :, d, :, j].rearrange("p a e f -> p a f e"),
+                            func=ACT.Copy,
+                            scale=tab[:, s, 0, 32 * d + j : 32 * d + j + 1],
+                        )
+
+            def add(n):
+                grp = groups[n]
+                k = grp["store"]
+                slots = [i % SLOTS - STORES[k][1] for i in grp["banks"]]
+                step = slots[-1] - slots[0] if len(slots) > 1 else 1
+                dest = res[k][:, :, slots[0] : slots[-1] + 1 : step, :]
+                engine = nc.vector if grp["banks"][-1] in V_ADDS else nc.gpsimd
+                if grp["scalar"]:
+                    engine.tensor_tensor(
+                        out=dest.rearrange("p (a e) s (d f j) -> p a e s d f j", e=2, d=2, f=2),
+                        in0=grp["ap"][:].rearrange("p a s (d f j) e -> p a e s d f j", d=2, f=2),
+                        in1=grp["bs"][:].rearrange("p (a e) s (d f j) -> p a e s d f j", e=2, d=2, f=2)[:, :, :, :, :, ::-1, :],
+                        op=ALU.add,
+                    )
+                else:
+                    ab6 = grp["ab"][:].rearrange("p r h s (d f j) -> p r h s d f j", d=2, f=2)
+                    parts = 2 if grp["banks"][-1] == BANKS - 1 else 1
+                    for h0 in range(0, 8, 8 // parts):
+                        h1 = h0 + 8 // parts
+                        engine.tensor_tensor(
+                            out=dest.rearrange("p h s (d f j) -> p h s d f j", d=2, f=2)[:, h0:h1],
+                            in0=ab6[:, 0, h0:h1],
+                            in1=ab6[:, 1, h0:h1, :, :, ::-1, :],
+                            op=ALU.add,
+                        )
+                        if parts > 1:
+                            store(k, h0, h1)
+                    if parts > 1:
+                        return
+                if last_add[k] == n:
+                    if STORES[k][2] == SLOTS:
+                        store(k, 0, 4)
+                        store(k, 4, 8)
+                    else:
+                        store(k, 0, 8)
 
             def store(k, h0, h1):
                 q, s0, n = STORES[k]
@@ -152,6 +224,12 @@ def tile_asymetrickernel_pb_kernel(tc, u_x, pos_x, Wq_words, Wq_scales, out):
                 nc.scalar.activation(out=tab6[:, s0:s1, 1, :, 0, :], in_=fr[:, 1, s0:s1], func=ACT.Sin, scale=2.0 * math.pi)
                 nc.scalar.activation(out=tab6[:, s0:s1, 1, :, 1, :], in_=fr[:, 1, s0:s1], func=ACT.Sin, scale=-2.0 * math.pi)
 
+            idle = psum_v.tile([P, 512], F32, name="idle", tag="acc")
+
+            def keep_warm(n):
+                for r in range(n):
+                    nc.tensor.matmul(out=idle[:], lhsT=dummy[:, 0:P], rhs=dummy[:], start=True, stop=True)
+
             pairs = {}
 
             def prepare(t):
@@ -159,8 +237,11 @@ def tile_asymetrickernel_pb_kernel(tc, u_x, pos_x, Wq_words, Wq_scales, out):
                     pairs[t // 2] = new_pair()
                 transpose(t, pairs[t // 2][:, t % 2, :])
 
+            keep_warm(3)
             prepare(0)
+            keep_warm(2)
             prepare(1)
+            keep_warm(2)
 
             for j in range(16):
                 nc.vector.tensor_scalar(
@@ -179,35 +260,36 @@ def tile_asymetrickernel_pb_kernel(tc, u_x, pos_x, Wq_words, Wq_scales, out):
             prepare(2)
             sines(2, 4)
 
-            adds = list(ADDS)
-            left = 0
-            for i in range(BANKS):
-                q, s = divmod(i, SLOTS)
-                t = (q // 2) * SLOTS + s
-                acc = multiply(t, q % 2)
-                if i == 0:
-                    prepare(3)
-                    sines(4, SLOTS)
-                if i + 4 < TILES:
-                    prepare(i + 4)
-                if i < 4:
-                    quantize(i + 2, 1, pairs[(i + 2) // 2][:, i % 2, :])
-                elif i + 2 < TILES and i % 2 == 0:
-                    quantize(i + 2, 2, pairs[i // 2 + 1][:].rearrange("p a c -> p (a c)"))
-                if left == 0:
-                    width, who = adds.pop(0)
-                    left = width
-                    first = s
-                    ab = prod.tile([P, 2, 8, width, 64], F32, name="ab", tag="ab")
-                products(ab, s - first, s, acc)
-                left -= 1
-                if left == 0:
-                    k = [n for n, (sq, s0, sn) in enumerate(STORES) if sq == q and s0 <= s < s0 + sn][0]
-                    s0 = STORES[k][1]
-                    add(nc.vector if who == "v" else nc.gpsimd, ab, res[k][:, :, first - s0 : s + 1 - s0, :])
-                    if s + 1 == s0 + STORES[k][2]:
-                        if STORES[k][2] == SLOTS:
-                            store(k, 0, 4)
-                            store(k, 4, 8)
-                        else:
-                            store(k, 0, 8)
+            for i in range(BANKS + LAG):
+                if i < BANKS:
+                    q, s = divmod(i, SLOTS)
+                    t = (q // 2) * SLOTS + s
+                    grp = groups[group_of[i]]
+                    acc = multiply(t, q % 2, psum_a if grp["scalar"] else psum_v)
+                    if i == 0:
+                        prepare(3)
+                        sines(4, SLOTS)
+                    if i + 4 < TILES:
+                        prepare(i + 4)
+                    if i < 4:
+                        quantize(i + 2, 1, pairs[(i + 2) // 2][:, i % 2, :])
+                    elif i + 2 < TILES and i % 2 == 0:
+                        quantize(i + 2, 2, pairs[i // 2 + 1][:].rearrange("p a c -> p (a c)"))
+                    width = len(grp["banks"])
+                    k = grp["banks"].index(i)
+                    if grp["scalar"]:
+                        if k == 0:
+                            ap = prod.tile([P, 4, width, 64, 2], F32, name="ap", tag="ap")
+                            bs = prod.tile([P, 8, width, 64], F32, name="bs", tag="bs")
+                            grp["ap"] = ap
+                            grp["bs"] = bs
+                        sine_product(grp["bs"], k, s, acc)
+                        cosine_product(grp["ap"], k, s, acc)
+                    else:
+                        if k == 0:
+                            ab = prod.tile([P, 2, 8, width, 64], F32, name="ab", tag="ab")
+                            grp["ab"] = ab
+                        both_products(grp["ab"], k, s, acc)
+                for n, grp in enumerate(groups):
+                    if grp["when"] == i:
+                        add(n)

@@ -22,10 +22,13 @@ TILES = 16
 BANKS = 32
 
 STORES = [(0, 0, 8), (1, 0, 8), (2, 0, 4), (2, 4, 4), (3, 0, 2), (3, 2, 2), (3, 4, 2), (3, 6, 1), (3, 7, 1)]
-A_BANKS = []
-V_ADDS = [30,31]
-ALONE = [0,1]
+A_BANKS = [12, 16, 20, 24, 27]
+V_ADDS = [17, 18, 25, 30, 31]
+ALONE = [0, 1] + A_BANKS
 LAG = 0
+S_FROM = 8
+S_EARLY = 5
+S_LATE = 9
 
 
 def tile_asymetrickernel_pb_kernel(tc, u_x, pos_x, Wq_words, Wq_scales, out):
@@ -119,7 +122,11 @@ def tile_asymetrickernel_pb_kernel(tc, u_x, pos_x, Wq_words, Wq_scales, out):
                     in_=xt[:].rearrange("p (g u) r -> p g r u", u=2),
                 )
 
+            quantized = set()
+
             def quantize(t, n, grouped):
+                for t2 in range(t, t + n):
+                    quantized.add(t2)
                 nc.vector.quantize_mx(
                     out=codes[:, t : t + n, :].rearrange("p a c -> p (a c)").bitcast(E5X4),
                     scales=xscale[:, t : t + n, :].rearrange("p a c -> p (a c)"),
@@ -130,8 +137,8 @@ def tile_asymetrickernel_pb_kernel(tc, u_x, pos_x, Wq_words, Wq_scales, out):
                 pair = stage.tile([P, 2, 1024], BF16, name="pair", tag="pair", align_bytes=64)
                 return pair
 
-            def multiply(t, nh, pool):
-                acc = pool.tile([P, 512], F32, name="acc", tag="acc")
+            def multiply(t, nh, pool, tag="acc"):
+                acc = pool.tile([P, 512], F32, name="acc", tag=tag)
                 for g in range(2):
                     nc.tensor.matmul_mx(
                         out=acc[:],
@@ -160,17 +167,37 @@ def tile_asymetrickernel_pb_kernel(tc, u_x, pos_x, Wq_words, Wq_scales, out):
                     op=ALU.mult,
                 )
 
-            def cosine_product(ap, k, s, acc):
+            def cosine_job(ap, s, acc, d, j):
                 ap7 = ap[:].rearrange("p a s (d f j) e -> p a s d f j e", d=2, f=2)
                 acc6 = acc[:].rearrange("p (a e d f j) -> p a e d f j", e=2, d=2, f=2, j=16)
-                for d in range(2):
-                    for j in range(16):
-                        nc.scalar.activation(
-                            out=ap7[:, :, k, d, :, j, :],
-                            in_=acc6[:, :, :, d, :, j].rearrange("p a e f -> p a f e"),
-                            func=ACT.Copy,
-                            scale=tab[:, s, 0, 32 * d + j : 32 * d + j + 1],
-                        )
+                nc.scalar.activation(
+                    out=ap7[:, :, 0, d, :, j, :],
+                    in_=acc6[:, :, :, d, :, j].rearrange("p a e f -> p a f e"),
+                    func=ACT.Copy,
+                    scale=tab[:, s, 0, 32 * d + j : 32 * d + j + 1],
+                )
+
+            jobs = [(b, d, j) for b in A_BANKS for d in range(2) for j in range(16)]
+            own_acc = {}
+
+            def hand_out(budget, only=None):
+                n = 0
+                while jobs and n < budget and (only is None or jobs[0][0] == only):
+                    b, d, j = jobs[0]
+                    bq, bs_ = divmod(b, SLOTS)
+                    bt = (bq // 2) * SLOTS + bs_
+                    if b not in own_acc:
+                        if bt not in quantized:
+                            return
+                        ap = prod.tile([P, 4, 1, 64, 2], F32, name="ap", tag="ap")
+                        groups[group_of[b]]["ap"] = ap
+                        if len(prepared) < TILES:
+                            own_acc[b] = multiply(bt, bq % 2, psum_a)
+                        else:
+                            own_acc[b] = multiply(bt, bq % 2, psum_t, "xt")
+                    cosine_job(groups[group_of[b]]["ap"], bs_, own_acc[b], d, j)
+                    jobs.remove(jobs[0])
+                    n += 1
 
             def add(n):
                 grp = groups[n]
@@ -232,7 +259,10 @@ def tile_asymetrickernel_pb_kernel(tc, u_x, pos_x, Wq_words, Wq_scales, out):
 
             pairs = {}
 
+            prepared = []
+
             def prepare(t):
+                prepared.append(t)
                 if t % 2 == 0:
                     pairs[t // 2] = new_pair()
                 transpose(t, pairs[t // 2][:, t % 2, :])
@@ -265,7 +295,7 @@ def tile_asymetrickernel_pb_kernel(tc, u_x, pos_x, Wq_words, Wq_scales, out):
                     q, s = divmod(i, SLOTS)
                     t = (q // 2) * SLOTS + s
                     grp = groups[group_of[i]]
-                    acc = multiply(t, q % 2, psum_a if grp["scalar"] else psum_v)
+                    acc = multiply(t, q % 2, psum_v)
                     if i == 0:
                         prepare(3)
                         sines(4, SLOTS)
@@ -277,14 +307,13 @@ def tile_asymetrickernel_pb_kernel(tc, u_x, pos_x, Wq_words, Wq_scales, out):
                         quantize(i + 2, 2, pairs[i // 2 + 1][:].rearrange("p a c -> p (a c)"))
                     width = len(grp["banks"])
                     k = grp["banks"].index(i)
+                    if i >= S_FROM:
+                        hand_out(S_EARLY if i + 4 < TILES else S_LATE)
                     if grp["scalar"]:
-                        if k == 0:
-                            ap = prod.tile([P, 4, width, 64, 2], F32, name="ap", tag="ap")
-                            bs = prod.tile([P, 8, width, 64], F32, name="bs", tag="bs")
-                            grp["ap"] = ap
-                            grp["bs"] = bs
+                        hand_out(32, i)
+                        bs = prod.tile([P, 8, width, 64], F32, name="bs", tag="bs")
+                        grp["bs"] = bs
                         sine_product(grp["bs"], k, s, acc)
-                        cosine_product(grp["ap"], k, s, acc)
                     else:
                         if k == 0:
                             ab = prod.tile([P, 2, 8, width, 64], F32, name="ab", tag="ab")

@@ -19,11 +19,15 @@ FLOPS = 2 * 2048 * 1024 * 1024
 P = 128
 SLOTS = 8
 TILES = 16
-BANKS = 32
+BANKS = 28
+TURNED = 4
+Q_FIRST = 12
 
-STORES = [(0, 0, 8), (1, 0, 8), (2, 0, 4), (2, 4, 4), (3, 0, 2), (3, 2, 2), (3, 4, 2), (3, 6, 1), (3, 7, 1)]
-A_BANKS = [12, 16, 20, 24, 27]
-V_ADDS = [17, 18, 25, 30, 31]
+STORES = [(0, 0, 8), (1, 0, 8), (2, 0, 4), (2, 4, 4), (3, 0, 2), (3, 2, 1), (3, 3, 1)]
+A_BANKS = [12, 16, 20, 24]
+V_ADDS = [26, 27]
+LINE = list(range(15)) + [-1, 15, 16, 17, -2, 18, 19, 20, -3, 21, 22, 23, -4, 24, 25, 26, 27]
+AHEAD_FROM = 13
 ALONE = [0, 1] + A_BANKS
 LAG = 0
 S_FROM = 8
@@ -53,7 +57,12 @@ def tile_asymetrickernel_pb_kernel(tc, u_x, pos_x, Wq_words, Wq_scales, out):
         turns = keep.tile([P, 2, 16, 16], F32, name="turns")
         whole = keep.tile([P, 2, 16, 16], I32, name="whole")
         frac = keep.tile([P, 2, 16, 16], F32, name="frac")
-        tab = keep.tile([P, SLOTS, 2, 64], F32, name="tab")
+        tab = keep.tile([P, SLOTS, 3, 64], F32, name="tab")
+        codes_q = keep.tile([P, 2, 512], U32, name="codes_q", align_bytes=64)
+        xscale_q = keep.tile([P, 2, 512], U8, name="xscale_q", align_bytes=64)
+        tab_t = keep.tile([P, 2, 512], F32, name="tab_t")
+        perm = [keep.tile([P, P], F32, name="perm%d" % w) for w in range(2)]
+        res_q = [keep.tile([P, 2, 4, 64], F32, name="res_q%d" % c) for c in range(TURNED)]
         dummy = keep.tile([P, 512], BF16, name="dummy")
         zero = keep.tile([P, 1], F32, name="zero")
         warm = keep.tile([P, 1], F32, name="warm")
@@ -86,6 +95,16 @@ def tile_asymetrickernel_pb_kernel(tc, u_x, pos_x, Wq_words, Wq_scales, out):
             nc.vector.memset(plane[:].bitcast(I32), 0)
             nc.gpsimd.memset(zero[:], 0.0)
             nc.scalar.activation(out=warm[:], in_=zero[:], func=ACT.Sin)
+            for w in range(2):
+                for half in range(2):
+                    cols = slice(64 * half, 64 * (half + 1))
+                    if half == w:
+                        nc.vector.tensor_copy(out=perm[w][:, cols], in_=ident[:, cols])
+                    else:
+                        nc.vector.tensor_copy(
+                            out=perm[w][:, cols].rearrange("p (d f j) -> p d f j", d=2, f=2),
+                            in_=ident[:, cols].rearrange("p (d f j) -> p d f j", d=2, f=2)[:, :, ::-1, :],
+                        )
 
             def load_x(t):
                 b, s = divmod(t, SLOTS)
@@ -118,7 +137,7 @@ def tile_asymetrickernel_pb_kernel(tc, u_x, pos_x, Wq_words, Wq_scales, out):
                     for u in range(2):
                         nc.tensor.transpose(xt[:, 2 * g + u, :], words[:, 256 * g + u : 256 * (g + 1) : 2], ident[:])
                 nc.scalar.copy(
-                    out=grouped.bitcast(F32).rearrange("p (g r u) -> p g r u", g=2, u=2),
+                    out=grouped.bitcast(F32).rearrange("p g (r u) -> p g r u", u=2),
                     in_=xt[:].rearrange("p (g u) r -> p g r u", u=2),
                 )
 
@@ -127,6 +146,15 @@ def tile_asymetrickernel_pb_kernel(tc, u_x, pos_x, Wq_words, Wq_scales, out):
             def quantize(t, n, grouped):
                 for t2 in range(t, t + n):
                     quantized.add(t2)
+                if t >= Q_FIRST:
+                    for g in range(2):
+                        cols = slice(128 * (t - Q_FIRST), 128 * (t - Q_FIRST + n))
+                        nc.vector.quantize_mx(
+                            out=codes_q[:, g, cols].bitcast(E5X4),
+                            scales=xscale_q[:, g, cols],
+                            in_=grouped[:, 1024 * g : 1024 * (g + 1)],
+                        )
+                    return
                 nc.vector.quantize_mx(
                     out=codes[:, t : t + n, :].rearrange("p a c -> p (a c)").bitcast(E5X4),
                     scales=xscale[:, t : t + n, :].rearrange("p a c -> p (a c)"),
@@ -140,10 +168,11 @@ def tile_asymetrickernel_pb_kernel(tc, u_x, pos_x, Wq_words, Wq_scales, out):
             def multiply(t, nh, pool, tag="acc"):
                 acc = pool.tile([P, 512], F32, name="acc", tag=tag)
                 for g in range(2):
+                    cols = slice(128 * (t - Q_FIRST), 128 * (t - Q_FIRST + 1))
                     nc.tensor.matmul_mx(
                         out=acc[:],
-                        lhsT=codes[:, t, 128 * g : 128 * (g + 1)].bitcast(E5X4),
-                        lhsT_scale=xscale[:, t, 128 * g : 128 * (g + 1)],
+                        lhsT=(codes_q[:, g, cols] if t >= Q_FIRST else codes[:, t, 128 * g : 128 * (g + 1)]).bitcast(E5X4),
+                        lhsT_scale=(xscale_q[:, g, cols] if t >= Q_FIRST else xscale[:, t, 128 * g : 128 * (g + 1)]),
                         rhs=w_half[nh][:, g, :].bitcast(E2X4),
                         rhs_scale=plane[:, g, 512 * nh : 512 * (nh + 1)],
                         start=(g == 0),
@@ -151,11 +180,63 @@ def tile_asymetrickernel_pb_kernel(tc, u_x, pos_x, Wq_words, Wq_scales, out):
                     )
                 return acc
 
+            def multiply_turned(c):
+                acc = psum_v.tile([P, 512], F32, name="acc", tag="acc")
+                for g in range(2):
+                    nc.tensor.matmul_mx(
+                        out=acc[:],
+                        lhsT=w_half[1][:, g, 256 * c : 256 * (c + 1)].bitcast(E2X4),
+                        lhsT_scale=plane[:, g, 512 + 128 * c : 512 + 128 * (c + 1)],
+                        rhs=codes_q[:, g, :].bitcast(E5X4),
+                        rhs_scale=xscale_q[:, g, :],
+                        start=(g == 0),
+                        stop=(g == 1),
+                    )
+                return acc
+
+            def turned_tables():
+                for w in range(2):
+                    xt = psum_t.tile([P, 4, P], F32, name="xt", tag="xt")
+                    for sl in range(4):
+                        nc.tensor.transpose(xt[:, sl, :], tab[:, 4 + sl, w : w + 2, :].rearrange("p r c -> p (r c)"), ident[:])
+                    nc.scalar.copy(out=tab_t[:, w, :], in_=xt[:].rearrange("p a b -> p (a b)"))
+
+            def turned_products(acc):
+                abt = prod.tile([P, 2, 512], F32, name="abt", tag="abt")
+                nc.vector.tensor_tensor(
+                    out=abt[:],
+                    in0=acc[:].rearrange("p (o n) -> p o n", o=1).to_broadcast([P, 2, 512]),
+                    in1=tab_t[:],
+                    op=ALU.mult,
+                )
+                return abt
+
+            def turn_back(c, abt):
+                ot = psum_t.tile([P, 4, P], F32, name="xt", tag="xt")
+                for sl in range(4):
+                    for w in range(2):
+                        nc.tensor.matmul(
+                            out=ot[:, sl, :],
+                            lhsT=abt[:, w, 128 * sl : 128 * (sl + 1)],
+                            rhs=perm[w][:],
+                            is_transpose=True,
+                            start=(w == 0),
+                            stop=(w == 1),
+                        )
+                nc.scalar.copy(
+                    out=res_q[c][:].rearrange("p h s c -> p s h c"),
+                    in_=ot[:].rearrange("p s (h c) -> p s h c", c=64),
+                )
+                nc.sync.dma_start(
+                    out=out[1, 8 + 2 * c : 10 + 2 * c].rearrange("h (p s) c -> p h s c", s=SLOTS)[:, :, 4:8, :],
+                    in_=res_q[c][:],
+                )
+
             def both_products(ab, k, s, acc):
                 nc.vector.tensor_tensor(
                     out=ab[:, :, :, k, :],
                     in0=acc[:].rearrange("p (o h c) -> p o h c", o=1, c=64).to_broadcast([P, 2, 8, 64]),
-                    in1=tab[:, s].unsqueeze(2).to_broadcast([P, 2, 8, 64]),
+                    in1=tab[:, s, 0:2].unsqueeze(2).to_broadcast([P, 2, 8, 64]),
                     op=ALU.mult,
                 )
 
@@ -191,10 +272,7 @@ def tile_asymetrickernel_pb_kernel(tc, u_x, pos_x, Wq_words, Wq_scales, out):
                             return
                         ap = prod.tile([P, 4, 1, 64, 2], F32, name="ap", tag="ap")
                         groups[group_of[b]]["ap"] = ap
-                        if len(prepared) < TILES:
-                            own_acc[b] = multiply(bt, bq % 2, psum_a)
-                        else:
-                            own_acc[b] = multiply(bt, bq % 2, psum_t, "xt")
+                        own_acc[b] = multiply(bt, bq % 2, psum_a)
                     cosine_job(groups[group_of[b]]["ap"], bs_, own_acc[b], d, j)
                     jobs.remove(jobs[0])
                     n += 1
@@ -248,6 +326,8 @@ def tile_asymetrickernel_pb_kernel(tc, u_x, pos_x, Wq_words, Wq_scales, out):
                 fr = frac[:].rearrange("p k (s d) j -> p k s d j", d=2)
                 for f in range(2):
                     nc.scalar.activation(out=tab6[:, s0:s1, 0, :, f, :], in_=fr[:, 0, s0:s1], func=ACT.Sin, scale=2.0 * math.pi)
+                    if s0 >= 4:
+                        nc.scalar.activation(out=tab6[:, s0:s1, 2, :, f, :], in_=fr[:, 0, s0:s1], func=ACT.Sin, scale=2.0 * math.pi)
                 nc.scalar.activation(out=tab6[:, s0:s1, 1, :, 0, :], in_=fr[:, 1, s0:s1], func=ACT.Sin, scale=2.0 * math.pi)
                 nc.scalar.activation(out=tab6[:, s0:s1, 1, :, 1, :], in_=fr[:, 1, s0:s1], func=ACT.Sin, scale=-2.0 * math.pi)
 
@@ -265,7 +345,10 @@ def tile_asymetrickernel_pb_kernel(tc, u_x, pos_x, Wq_words, Wq_scales, out):
                 prepared.append(t)
                 if t % 2 == 0:
                     pairs[t // 2] = new_pair()
-                transpose(t, pairs[t // 2][:, t % 2, :])
+                if t >= Q_FIRST:
+                    transpose(t, pairs[t // 2][:].rearrange("p g (a c) -> p g a c", a=2)[:, :, t % 2, :])
+                else:
+                    transpose(t, pairs[t // 2][:, t % 2, :].rearrange("p (g c) -> p g c", g=2))
 
             keep_warm(3)
             prepare(0)
@@ -290,12 +373,35 @@ def tile_asymetrickernel_pb_kernel(tc, u_x, pos_x, Wq_words, Wq_scales, out):
             prepare(2)
             sines(2, 4)
 
-            for i in range(BANKS + LAG):
-                if i < BANKS:
+            accs = {}
+            waiting = []
+
+            def need(n):
+                if n < len(LINE) and n not in accs:
+                    if LINE[n] < 0:
+                        accs[n] = multiply_turned(-1 - LINE[n])
+                    else:
+                        accs[n] = multiply((LINE[n] // 16) * SLOTS + LINE[n] % SLOTS, (LINE[n] // SLOTS) % 2, psum_v)
+
+            for n_line, i in enumerate(LINE):
+                need(n_line)
+                if n_line >= AHEAD_FROM:
+                    need(n_line + 1)
+                    need(n_line + 2)
+                    need(n_line + 3)
+                for c, abt in waiting:
+                    turn_back(c, abt)
+                waiting.clear()
+                if i == 12:
+                    turned_tables()
+                if i < 0:
+                    hand_out(S_LATE)
+                    waiting.append((-1 - i, turned_products(accs[n_line])))
+                else:
                     q, s = divmod(i, SLOTS)
                     t = (q // 2) * SLOTS + s
                     grp = groups[group_of[i]]
-                    acc = multiply(t, q % 2, psum_v)
+                    acc = accs[n_line]
                     if i == 0:
                         prepare(3)
                         sines(4, SLOTS)
@@ -322,3 +428,5 @@ def tile_asymetrickernel_pb_kernel(tc, u_x, pos_x, Wq_words, Wq_scales, out):
                 for n, grp in enumerate(groups):
                     if grp["when"] == i:
                         add(n)
+            for c, abt in waiting:
+                turn_back(c, abt)

@@ -24,7 +24,7 @@ TURNED = 4
 Q_FIRST = 12
 
 STORES = [(0, 0, 8), (1, 0, 8), (2, 0, 4), (2, 4, 4), (3, 0, 2), (3, 2, 1), (3, 3, 1)]
-A_BANKS = [12, 16, 20, 24]
+A_BANKS = [12, 15, 18, 21, 24]
 V_ADDS = [26, 27]
 LINE = list(range(15)) + [-1, 15, 16, 17, -2, 18, 19, 20, -3, 21, 22, 23, -4, 24, 25, 26, 27]
 AHEAD_FROM = 13
@@ -32,7 +32,7 @@ ALONE = [0, 1] + A_BANKS
 LAG = 0
 S_FROM = 8
 S_EARLY = 5
-S_LATE = 9
+S_LATE = 10
 
 
 def tile_asymetrickernel_pb_kernel(tc, u_x, pos_x, Wq_words, Wq_scales, out):

@@ -42,8 +42,8 @@ def tile_asymetrickernel_pb_kernel(tc, u_x, pos_x, Wq_words, Wq_scales, out):
         stage = ctx.enter_context(tc.tile_pool(name="stage", bufs=4))
         prod = ctx.enter_context(tc.tile_pool(name="prod", bufs=3))
         psum_t = ctx.enter_context(tc.psum_pool(name="psum_t", bufs=2))
-        psum_v = ctx.enter_context(tc.psum_pool(name="psum_v", bufs=5))
-        psum_a = ctx.enter_context(tc.psum_pool(name="psum_a", bufs=1))
+        psum_v = ctx.enter_context(tc.psum_pool(name="psum_v", bufs=4))
+        psum_a = ctx.enter_context(tc.psum_pool(name="psum_a", bufs=2))
 
         ident = keep.tile([P, P], F32, name="ident")
         make_identity(nc, ident[:])

@@ -25,7 +25,7 @@ Q_FIRST = 12
 
 STORES = [(0, 0, 8), (1, 0, 8), (2, 0, 4), (2, 4, 4), (3, 0, 2), (3, 2, 1), (3, 3, 1)]
 A_BANKS = [12, 15, 18, 21, 24]
-V_ADDS = [26, 27]
+V_ADDS = [25, 26, 27]
 LINE = list(range(15)) + [-1, 15, 16, 17, -2, 18, 19, 20, -3, 21, 22, 23, -4, 24, 25, 26, 27]
 AHEAD_FROM = 13
 ALONE = [0, 1] + A_BANKS

import math
from contextlib import ExitStack

import concourse.mybir as mybir
from concourse.masks import make_identity

F32 = mybir.dt.float32
BF16 = mybir.dt.bfloat16
I32 = mybir.dt.int32
U32 = mybir.dt.uint32
U8 = mybir.dt.uint8
E5X4 = mybir.dt.float8_e5m2_x4
E2X4 = mybir.dt.float4_e2m1fn_x4
ALU = mybir.AluOpType
ACT = mybir.ActivationFunctionType

FLOPS = 2 * 2048 * 1024 * 1024

P = 128
SLOTS = 8
TILES = 16
BANKS = 28
TURNED = 4
Q_FIRST = 12

STORES = [(0, 0, 8), (1, 0, 8), (2, 0, 4), (2, 4, 4), (3, 0, 2), (3, 2, 1), (3, 3, 1)]
A_BANKS = [12, 15, 18, 21, 24]
V_ADDS = [25, 26, 27]
LINE = list(range(15)) + [-1, 15, 16, 17, -2, 18, 19, 20, -3, 21, 22, 23, -4, 24, 25, 26, 27]
AHEAD_FROM = 13
ALONE = [0, 1] + A_BANKS
LAG = 0
S_FROM = 8
S_EARLY = 5
S_LATE = 10


def tile_asymetrickernel_pb_kernel(tc, u_x, pos_x, Wq_words, Wq_scales, out):
    nc = tc.nc
    with ExitStack() as ctx:
        keep = ctx.enter_context(tc.tile_pool(name="keep", bufs=1))
        stage = ctx.enter_context(tc.tile_pool(name="stage", bufs=4))
        prod = ctx.enter_context(tc.tile_pool(name="prod", bufs=3))
        psum_t = ctx.enter_context(tc.psum_pool(name="psum_t", bufs=2))
        psum_v = ctx.enter_context(tc.psum_pool(name="psum_v", bufs=4))
        psum_a = ctx.enter_context(tc.psum_pool(name="psum_a", bufs=2))

        ident = keep.tile([P, P], F32, name="ident")
        make_identity(nc, ident[:])

        plane = keep.tile([P, 2, 1024], U8, name="plane", align_bytes=64)
        w_half = [keep.tile([P, 2, 1024], U8, name="w_half%d" % nh, align_bytes=64) for nh in range(2)]
        pos = keep.tile([P, 16], BF16, name="pos")
        x_sb = [keep.tile([P, 1024], BF16, name="x_sb%d" % t, align_bytes=64) for t in range(TILES)]
        codes = keep.tile([P, TILES, 256], U32, name="codes", align_bytes=64)
        xscale = keep.tile([P, TILES, 256], U8, name="xscale", align_bytes=64)
        turns = keep.tile([P, 2, 16, 16], F32, name="turns")
        whole = keep.tile([P, 2, 16, 16], I32, name="whole")
        frac = keep.tile([P, 2, 16, 16], F32, name="frac")
        tab = keep.tile([P, SLOTS, 3, 64], F32, name="tab")
        codes_q = keep.tile([P, 2, 512], U32, name="codes_q", align_bytes=64)
        xscale_q = keep.tile([P, 2, 512], U8, name="xscale_q", align_bytes=64)
        tab_t = keep.tile([P, 2, 512], F32, name="tab_t")
        perm = [keep.tile([P, P], F32, name="perm%d" % w) for w in range(2)]
        res_q = [keep.tile([P, 2, 4, 64], F32, name="res_q%d" % c) for c in range(TURNED)]
        dummy = keep.tile([P, 512], BF16, name="dummy")
        zero = keep.tile([P, 1], F32, name="zero")
        warm = keep.tile([P, 1], F32, name="warm")
        res = [keep.tile([P, 8, n, 64], F32, name="res%d" % k) for k, (q, s0, n) in enumerate(STORES)]

        groups = []
        open_group = {}
        for i in range(BANKS):
            q, s = divmod(i, SLOTS)
            k = [n for n, (sq, s0, sn) in enumerate(STORES) if sq == q and s0 <= s < s0 + sn][0]
            key = (k, i in A_BANKS)
            if key in open_group and i not in ALONE:
                groups[open_group.pop(key)]["banks"].append(i)
            else:
                if i not in ALONE:
                    open_group[key] = len(groups)
                groups.append({"banks": [i], "store": k, "scalar": i in A_BANKS})
        group_of = {}
        for n, grp in enumerate(groups):
            for i in grp["banks"]:
                group_of[i] = n
        last_add = {}
        for n, grp in enumerate(groups):
            grp["when"] = grp["banks"][-1] + (LAG if grp["scalar"] else 0)
        for n in sorted(range(len(groups)), key=lambda m: (groups[m]["when"], m)):
            last_add[groups[n]["store"]] = n

        with tc.manual_schedule():
            nc.vector.memset(dummy[:], 0.0)
            nc.vector.memset(plane[:].bitcast(I32), 0)
            nc.gpsimd.memset(zero[:], 0.0)
            nc.scalar.activation(out=warm[:], in_=zero[:], func=ACT.Sin)
            for w in range(2):
                for half in range(2):
                    cols = slice(64 * half, 64 * (half + 1))
                    if half == w:
                        nc.vector.tensor_copy(out=perm[w][:, cols], in_=ident[:, cols])
                    else:
                        nc.vector.tensor_copy(
                            out=perm[w][:, cols].rearrange("p (d f j) -> p d f j", d=2, f=2),
                            in_=ident[:, cols].rearrange("p (d f j) -> p d f j", d=2, f=2)[:, :, ::-1, :],
                        )

            def load_x(t):
                b, s = divmod(t, SLOTS)
                nc.sync.dma_start(out=x_sb[t][:], in_=u_x[b].rearrange("(p s) k -> p s k", s=SLOTS)[:, s, :])

            def load_w(nh):
                nc.sync.dma_start(
                    out=w_half[nh][:].bitcast(I32),
                    in_=Wq_words.rearrange("g p n -> p g n")[:, :, 1024 * nh : 1024 * (nh + 1)].bitcast(I32),
                )

            nc.sync.dma_start(out=pos[:], in_=pos_x[0].rearrange("(p s) d -> p (s d)", s=SLOTS))
            load_x(0)
            for q in range(4):
                nc.sync.dma_start(
                    out=plane[32 * q : 32 * q + 4, :, :].bitcast(I32),
                    in_=Wq_scales[:, 4 * q : 4 * q + 4, :].rearrange("g r n -> r g n").bitcast(I32),
                )
            load_w(0)
            for t in range(1, SLOTS):
                load_x(t)
            load_w(1)
            for t in range(SLOTS, TILES):
                load_x(t)

            def transpose(t, grouped):
                words = x_sb[t][:].bitcast(F32)
                xt = psum_t.tile([P, 4, P], F32, name="xt", tag="xt")
                for g in range(2):
                    for u in range(2):
                        nc.tensor.transpose(xt[:, 2 * g + u, :], words[:, 256 * g + u : 256 * (g + 1) : 2], ident[:])
                nc.scalar.copy(
                    out=grouped.bitcast(F32).rearrange("p g (r u) -> p g r u", u=2),
                    in_=xt[:].rearrange("p (g u) r -> p g r u", u=2),
                )

            quantized = set()

            def quantize(t, n, grouped):
                for t2 in range(t, t + n):
                    quantized.add(t2)
                if t >= Q_FIRST:
                    for g in range(2):
                        cols = slice(128 * (t - Q_FIRST), 128 * (t - Q_FIRST + n))
                        nc.vector.quantize_mx(
                            out=codes_q[:, g, cols].bitcast(E5X4),
                            scales=xscale_q[:, g, cols],
                            in_=grouped[:, 1024 * g : 1024 * (g + 1)],
                        )
                    return
                nc.vector.quantize_mx(
                    out=codes[:, t : t + n, :].rearrange("p a c -> p (a c)").bitcast(E5X4),
                    scales=xscale[:, t : t + n, :].rearrange("p a c -> p (a c)"),
                    in_=grouped,
                )

            def new_pair():
                pair = stage.tile([P, 2, 1024], BF16, name="pair", tag="pair", align_bytes=64)
                return pair

            def multiply(t, nh, pool, tag="acc"):
                acc = pool.tile([P, 512], F32, name="acc", tag=tag)
                for g in range(2):
                    cols = slice(128 * (t - Q_FIRST), 128 * (t - Q_FIRST + 1))
                    nc.tensor.matmul_mx(
                        out=acc[:],
                        lhsT=(codes_q[:, g, cols] if t >= Q_FIRST else codes[:, t, 128 * g : 128 * (g + 1)]).bitcast(E5X4),
                        lhsT_scale=(xscale_q[:, g, cols] if t >= Q_FIRST else xscale[:, t, 128 * g : 128 * (g + 1)]),
                        rhs=w_half[nh][:, g, :].bitcast(E2X4),
                        rhs_scale=plane[:, g, 512 * nh : 512 * (nh + 1)],
                        start=(g == 0),
                        stop=(g == 1),
                    )
                return acc

            def multiply_turned(c):
                acc = psum_v.tile([P, 512], F32, name="acc", tag="acc")
                for g in range(2):
                    nc.tensor.matmul_mx(
                        out=acc[:],
                        lhsT=w_half[1][:, g, 256 * c : 256 * (c + 1)].bitcast(E2X4),
                        lhsT_scale=plane[:, g, 512 + 128 * c : 512 + 128 * (c + 1)],
                        rhs=codes_q[:, g, :].bitcast(E5X4),
                        rhs_scale=xscale_q[:, g, :],
                        start=(g == 0),
                        stop=(g == 1),
                    )
                return acc

            def turned_tables():
                for w in range(2):
                    xt = psum_t.tile([P, 4, P], F32, name="xt", tag="xt")
                    for sl in range(4):
                        nc.tensor.transpose(xt[:, sl, :], tab[:, 4 + sl, w : w + 2, :].rearrange("p r c -> p (r c)"), ident[:])
                    nc.scalar.copy(out=tab_t[:, w, :], in_=xt[:].rearrange("p a b -> p (a b)"))

            def turned_products(acc):
                abt = prod.tile([P, 2, 512], F32, name="abt", tag="abt")
                nc.vector.tensor_tensor(
                    out=abt[:],
                    in0=acc[:].rearrange("p (o n) -> p o n", o=1).to_broadcast([P, 2, 512]),
                    in1=tab_t[:],
                    op=ALU.mult,
                )
                return abt

            def turn_back(c, abt):
                ot = psum_t.tile([P, 4, P], F32, name="xt", tag="xt")
                for sl in range(4):
                    for w in range(2):
                        nc.tensor.matmul(
                            out=ot[:, sl, :],
                            lhsT=abt[:, w, 128 * sl : 128 * (sl + 1)],
                            rhs=perm[w][:],
                            is_transpose=True,
                            start=(w == 0),
                            stop=(w == 1),
                        )
                nc.scalar.copy(
                    out=res_q[c][:].rearrange("p h s c -> p s h c"),
                    in_=ot[:].rearrange("p s (h c) -> p s h c", c=64),
                )
                nc.sync.dma_start(
                    out=out[1, 8 + 2 * c : 10 + 2 * c].rearrange("h (p s) c -> p h s c", s=SLOTS)[:, :, 4:8, :],
                    in_=res_q[c][:],
                )

            def both_products(ab, k, s, acc):
                nc.vector.tensor_tensor(
                    out=ab[:, :, :, k, :],
                    in0=acc[:].rearrange("p (o h c) -> p o h c", o=1, c=64).to_broadcast([P, 2, 8, 64]),
                    in1=tab[:, s, 0:2].unsqueeze(2).to_broadcast([P, 2, 8, 64]),
                    op=ALU.mult,
                )

            def sine_product(bs, k, s, acc):
                nc.vector.tensor_tensor(
                    out=bs[:, :, k, :],
                    in0=acc[:].rearrange("p (h c) -> p h c", c=64),
                    in1=tab[:, s, 1:2, :].to_broadcast([P, 8, 64]),
                    op=ALU.mult,
                )

            def cosine_job(ap, s, acc, d, j):
                ap7 = ap[:].rearrange("p a s (d f j) e -> p a s d f j e", d=2, f=2)
                acc6 = acc[:].rearrange("p (a e d f j) -> p a e d f j", e=2, d=2, f=2, j=16)
                nc.scalar.activation(
                    out=ap7[:, :, 0, d, :, j, :],
                    in_=acc6[:, :, :, d, :, j].rearrange("p a e f -> p a f e"),
                    func=ACT.Copy,
                    scale=tab[:, s, 0, 32 * d + j : 32 * d + j + 1],
                )

            jobs = [(b, d, j) for b in A_BANKS for d in range(2) for j in range(16)]
            own_acc = {}

            def hand_out(budget, only=None):
                n = 0
                while jobs and n < budget and (only is None or jobs[0][0] == only):
                    b, d, j = jobs[0]
                    bq, bs_ = divmod(b, SLOTS)
                    bt = (bq // 2) * SLOTS + bs_
                    if b not in own_acc:
                        if bt not in quantized:
                            return
                        ap = prod.tile([P, 4, 1, 64, 2], F32, name="ap", tag="ap")
                        groups[group_of[b]]["ap"] = ap
                        own_acc[b] = multiply(bt, bq % 2, psum_a)
                    cosine_job(groups[group_of[b]]["ap"], bs_, own_acc[b], d, j)
                    jobs.remove(jobs[0])
                    n += 1

            def add(n):
                grp = groups[n]
                k = grp["store"]
                slots = [i % SLOTS - STORES[k][1] for i in grp["banks"]]
                step = slots[-1] - slots[0] if len(slots) > 1 else 1
                dest = res[k][:, :, slots[0] : slots[-1] + 1 : step, :]
                engine = nc.vector if grp["banks"][-1] in V_ADDS else nc.gpsimd
                if grp["scalar"]:
                    engine.tensor_tensor(
                        out=dest.rearrange("p (a e) s (d f j) -> p a e s d f j", e=2, d=2, f=2),
                        in0=grp["ap"][:].rearrange("p a s (d f j) e -> p a e s d f j", d=2, f=2),
                        in1=grp["bs"][:].rearrange("p (a e) s (d f j) -> p a e s d f j", e=2, d=2, f=2)[:, :, :, :, :, ::-1, :],
                        op=ALU.add,
                    )
                else:
                    ab6 = grp["ab"][:].rearrange("p r h s (d f j) -> p r h s d f j", d=2, f=2)
                    parts = 2 if grp["banks"][-1] == BANKS - 1 else 1
                    for h0 in range(0, 8, 8 // parts):
                        h1 = h0 + 8 // parts
                        engine.tensor_tensor(
                            out=dest.rearrange("p h s (d f j) -> p h s d f j", d=2, f=2)[:, h0:h1],
                            in0=ab6[:, 0, h0:h1],
                            in1=ab6[:, 1, h0:h1, :, :, ::-1, :],
                            op=ALU.add,
                        )
                        if parts > 1:
                            store(k, h0, h1)
                    if parts > 1:
                        return
                if last_add[k] == n:
                    if STORES[k][2] == SLOTS:
                        store(k, 0, 4)
                        store(k, 4, 8)
                    else:
                        store(k, 0, 8)

            def store(k, h0, h1):
                q, s0, n = STORES[k]
                b, nh = divmod(q, 2)
                nc.sync.dma_start(
                    out=out[b, 8 * nh + h0 : 8 * nh + h1].rearrange("h (p s) c -> p h s c", s=SLOTS)[:, :, s0 : s0 + n, :],
                    in_=res[k][:, h0:h1, :, :],
                )

            def sines(s0, s1):
                tab6 = tab[:].rearrange("p s r (d f j) -> p s r d f j", d=2, f=2)
                fr = frac[:].rearrange("p k (s d) j -> p k s d j", d=2)
                for f in range(2):
                    nc.scalar.activation(out=tab6[:, s0:s1, 0, :, f, :], in_=fr[:, 0, s0:s1], func=ACT.Sin, scale=2.0 * math.pi)
                    if s0 >= 4:
                        nc.scalar.activation(out=tab6[:, s0:s1, 2, :, f, :], in_=fr[:, 0, s0:s1], func=ACT.Sin, scale=2.0 * math.pi)
                nc.scalar.activation(out=tab6[:, s0:s1, 1, :, 0, :], in_=fr[:, 1, s0:s1], func=ACT.Sin, scale=2.0 * math.pi)
                nc.scalar.activation(out=tab6[:, s0:s1, 1, :, 1, :], in_=fr[:, 1, s0:s1], func=ACT.Sin, scale=-2.0 * math.pi)

            idle = psum_v.tile([P, 512], F32, name="idle", tag="acc")

            def keep_warm(n):
                for r in range(n):
                    nc.tensor.matmul(out=idle[:], lhsT=dummy[:, 0:P], rhs=dummy[:], start=True, stop=True)

            pairs = {}

            prepared = []

            def prepare(t):
                prepared.append(t)
                if t % 2 == 0:
                    pairs[t // 2] = new_pair()
                if t >= Q_FIRST:
                    transpose(t, pairs[t // 2][:].rearrange("p g (a c) -> p g a c", a=2)[:, :, t % 2, :])
                else:
                    transpose(t, pairs[t // 2][:, t % 2, :].rearrange("p (g c) -> p g c", g=2))

            keep_warm(3)
            prepare(0)
            keep_warm(2)
            prepare(1)
            keep_warm(2)

            for j in range(16):
                nc.vector.tensor_scalar(
                    out=turns[:, 1, :, j],
                    in0=pos[:],
                    scalar1=64.0 * 10000.0 ** (-j / 16.0) / (2.0 * math.pi),
                    scalar2=None,
                    op0=ALU.mult,
                )
            nc.vector.tensor_scalar(out=turns[:, 0], in0=turns[:, 1], scalar1=0.25, scalar2=None, op0=ALU.add)
            nc.vector.tensor_copy(out=whole[:], in_=turns[:])
            nc.vector.tensor_tensor(out=frac[:], in0=turns[:], in1=whole[:], op=ALU.subtract)
            quantize(0, 1, pairs[0][:, 0, :])
            quantize(1, 1, pairs[0][:, 1, :])
            sines(0, 2)
            prepare(2)
            sines(2, 4)

            accs = {}
            waiting = []

            def need(n):
                if n < len(LINE) and n not in accs:
                    if LINE[n] < 0:
                        accs[n] = multiply_turned(-1 - LINE[n])
                    else:
                        accs[n] = multiply((LINE[n] // 16) * SLOTS + LINE[n] % SLOTS, (LINE[n] // SLOTS) % 2, psum_v)

            for n_line, i in enumerate(LINE):
                need(n_line)
                if n_line >= AHEAD_FROM:
                    need(n_line + 1)
                    need(n_line + 2)
                    need(n_line + 3)
                for c, abt in waiting:
                    turn_back(c, abt)
                waiting.clear()
                if i == 12:
                    turned_tables()
                if i < 0:
                    hand_out(S_LATE)
                    waiting.append((-1 - i, turned_products(accs[n_line])))
                else:
                    q, s = divmod(i, SLOTS)
                    t = (q // 2) * SLOTS + s
                    grp = groups[group_of[i]]
                    acc = accs[n_line]
                    if i == 0:
                        prepare(3)
                        sines(4, SLOTS)
                    if i + 4 < TILES:
                        prepare(i + 4)
                    if i < 4:
                        quantize(i + 2, 1, pairs[(i + 2) // 2][:, i % 2, :])
                    elif i + 2 < TILES and i % 2 == 0:
                        quantize(i + 2, 2, pairs[i // 2 + 1][:].rearrange("p a c -> p (a c)"))
                    width = len(grp["banks"])
                    k = grp["banks"].index(i)
                    if i >= S_FROM:
                        hand_out(S_EARLY if i + 4 < TILES else S_LATE)
                    if grp["scalar"]:
                        hand_out(32, i)
                        bs = prod.tile([P, 8, width, 64], F32, name="bs", tag="bs")
                        grp["bs"] = bs
                        sine_product(grp["bs"], k, s, acc)
                    else:
                        if k == 0:
                            ab = prod.tile([P, 2, 8, width, 64], F32, name="ab", tag="ab")
                            grp["ab"] = ab
                        both_products(grp["ab"], k, s, acc)
                for n, grp in enumerate(groups):
                    if grp["when"] == i:
                        add(n)
            for c, abt in waiting:
                turn_back(c, abt)
